import numpy as np
import ml_dtypes


def mxq(x, axis, fmt="e4m3"):
    dtype, down = {"e4m3": (ml_dtypes.float8_e4m3fn, 7), "e5m2": (ml_dtypes.float8_e5m2, 14)}[fmt]
    v = np.moveaxis(np.asarray(x, np.float32).astype(ml_dtypes.bfloat16).astype(np.float64), axis, -1)
    blocks = v.reshape(v.shape[:-1] + (-1, 32))
    amax = np.abs(blocks).max(-1, keepdims=True)
    byte = np.maximum(np.where(amax > 0, np.frexp(amax)[1] - 1 + 127, 0) - down, 1)
    scale = np.exp2(byte - 127.0)
    codes = (blocks / scale).astype(np.float32).astype(dtype).astype(np.float64)
    return np.moveaxis((codes * scale).reshape(v.shape), -1, axis)


WIDE = False


def mx_kscale(k):
    if not WIDE:
        return np.ones(k)
    levels = np.array([10, -10, 5, -5, 0])
    a = np.random.permutation(np.resize(levels, k // 512 * 4)).reshape(k // 512, 4)
    idx = np.arange(k)
    return np.exp2(a[idx // 512, idx % 128 // 32])


BF16 = ml_dtypes.bfloat16


def bf(x):
    return np.asarray(x, np.float32).astype(BF16)


def f64(x):
    return np.asarray(x).astype(np.float64)


B, D0, D1, D2, D3 = 8192, 2048, 2048, 1024, 512
HEBB = 0.01
RATE = 0.001
BATCH_NUM = 1
C = HEBB * RATE / BATCH_NUM


def centred(s):
    return s / np.exp2(np.round(np.log2(s.mean())))


def setup_inputs():
    s = centred(mx_kscale(D2))
    return {"vi": bf(np.maximum(3.0 + 5.0 * np.random.standard_normal((B, D2)), 0.0) * s),
            "W": bf(np.random.standard_normal((D3, D2)) * 0.9 / np.sqrt(D2) / s[None, :]),
            "b": bf(3.0 + 1.5 * np.random.standard_normal(D3))}


def reference(vi, W, b):
    vi = f64(vi)
    vj = np.maximum((mxq(vi, 1, "e4m3") @ mxq(f64(W), 1, "e4m3").T) + f64(b), 0.0)
    m = np.mean(vj, axis=0)
    out = vj + np.sum(vi, axis=1, keepdims=True) * (C * m)[None, :]
    return out, m

@@ -1,0 +1,260 @@
+from contextlib import ExitStack
+
+import concourse.mybir as mybir
+from concourse.masks import make_identity
+
+F32 = mybir.dt.float32
+BF16 = mybir.dt.bfloat16
+U32 = mybir.dt.uint32
+U8 = mybir.dt.uint8
+FP8X4 = mybir.dt.float8_e4m3fn_x4
+ALU = mybir.AluOpType
+ACT = mybir.ActivationFunctionType
+AX = mybir.AxisListType
+
+P = 128
+ROWS = 8192
+K_IN = 1024
+OUTS = 512
+CHUNK = 512
+N_CHUNKS = ROWS // CHUNK
+SUB = CHUNK // P
+O_TILES = OUTS // P
+PASSES = K_IN // 512
+C_HEBB = 0.01 * 0.001 / 1
+FLOPS = 2 * ROWS * K_IN * OUTS
+
+X_BUFS = 7
+DEFERRED = 5
+ITEMS_PER_ITER = 3
+
+
+def tile_optimalnet_pb_t_kernel(tc, vi, W, b, out_0, out_1):
+    nc = tc.nc
+    vi_c = vi.rearrange("(c p t) k -> c p (t k)", p=P, t=SUB)
+    vi_ct = vi.rearrange("(c p t) k -> c t p k", p=P, t=SUB)
+    w_t = W.rearrange("(t p) k -> t p k", p=P)
+    out_c = out_0.rearrange("(c p t) o -> c p (t o)", p=P, t=SUB)
+    out_ct = out_0.rearrange("(c p t) o -> c t p o", p=P, t=SUB)
+
+    with ExitStack() as ctx:
+        const = ctx.enter_context(tc.tile_pool(name="const", bufs=1))
+        vjp = ctx.enter_context(tc.tile_pool(name="vjp", bufs=1))
+        xp = ctx.enter_context(tc.tile_pool(name="xp", bufs=X_BUFS))
+        gp = ctx.enter_context(tc.tile_pool(name="gp", bufs=2))
+        cp = ctx.enter_context(tc.tile_pool(name="cp", bufs=2))
+        ps = ctx.enter_context(tc.psum_pool(name="ps", bufs=4))
+        ctx.enter_context(tc.manual_schedule())
+
+        ident = const.tile([P, P], F32, name="ident")
+        bz = const.tile([P, P], BF16, name="bz")
+        bzf = const.tile([P, P], F32, name="bzf")
+        bias = const.tile([P, O_TILES], F32, name="bias")
+        acc = const.tile([P, O_TILES * N_CHUNKS], F32, name="acc")
+        msum = const.tile([P, O_TILES], F32, name="msum")
+        mean = const.tile([P, O_TILES], F32, name="mean")
+        mb = const.tile([P, OUTS], F32, name="mb")
+        rs_v = const.tile([P, N_CHUNKS * SUB], F32, name="rs_v")
+        rsc_v = const.tile([P, N_CHUNKS * SUB], F32, name="rsc_v")
+        rsc_s = const.tile([P, N_CHUNKS * SUB], F32, name="rsc_s")
+        junk_v = const.tile([P, K_IN], BF16, name="junk_v")
+        junk_s = const.tile([P, K_IN], BF16, name="junk_s")
+        w_codes = const.tile([P, PASSES * OUTS], U32, name="w_codes", align_bytes=64)
+        w_planes = const.tile([P, PASSES * OUTS], U8, name="w_planes", align_bytes=64)
+
+        make_identity(nc, ident[:])
+        nc.vector.memset(bz[:], 0.0)
+        nc.scalar.dma_start(out=bz[0:O_TILES, :], in_=b.rearrange("(t p) -> t p", p=P))
+
+        x_tiles = {}
+
+        def load(c):
+            x = xp.tile([P, SUB * K_IN], BF16, name="x%d" % c, tag="x")
+            x_tiles[c] = x
+            if c == 0:
+                for t in range(SUB):
+                    nc.sync.dma_start(out=x[:, t * K_IN : (t + 1) * K_IN], in_=vi_ct[c, t])
+            else:
+                nc.sync.dma_start(out=x[:], in_=vi_c[c])
+
+        def transposes(x):
+            x32 = x[:].bitcast(F32)
+            banks = []
+            for g in range(PASSES):
+                for tp in range(2):
+                    bank = ps.tile([P, 512], F32, name="tb", tag="T")
+                    for tt in range(2):
+                        t = 2 * tp + tt
+                        for u in range(2):
+                            col = 512 * t + 128 * (2 * g + u)
+                            nc.tensor.transpose(
+                                bank[:, 256 * u + 128 * tt : 256 * u + 128 * tt + 128],
+                                x32[:, col : col + 128],
+                                ident[:],
+                            )
+                    banks.append(bank)
+            return banks
+
+        def copy_out(engine, grouped, banks, j):
+            g32 = grouped[:].bitcast(F32)
+            dst = g32[:, 512 * j : 512 * j + 512].rearrange("p (c u) -> p c u", u=2)
+            src = banks[j][:].rearrange("p (u c) -> p c u", u=2)
+            if engine == "v":
+                nc.vector.tensor_copy(out=dst, in_=src)
+            else:
+                nc.scalar.copy(out=dst, in_=src)
+
+        def quantise(grouped, codes, planes):
+            nc.vector.quantize_mx(out=codes[:].bitcast(FP8X4), scales=planes[:], in_=grouped[:])
+
+        items = [(c, t) for c in range(N_CHUNKS - DEFERRED) for t in range(SUB)]
+        taken = [0]
+
+        def row_sums(n):
+            for q in range(n):
+                if taken[0] < len(items):
+                    c, t = items[taken[0]]
+                    taken[0] = taken[0] + 1
+                    nc.vector.tensor_scalar(
+                        out=junk_v[:],
+                        in0=x_tiles[c][:, t * K_IN : (t + 1) * K_IN],
+                        scalar1=1.0,
+                        scalar2=None,
+                        op0=ALU.mult,
+                        op1=ALU.add,
+                        accum_out=rs_v[:, SUB * c + t : SUB * c + t + 1],
+                    )
+
+        wx = xp.tile([P, SUB * K_IN], BF16, name="wx", tag="x")
+        for t in range(O_TILES):
+            nc.sync.dma_start(out=wx[:, t * K_IN : (t + 1) * K_IN], in_=w_t[t])
+        for c in range(X_BUFS - 1):
+            load(c)
+        w_banks = transposes(wx)
+        w_grouped = gp.tile([P, 4096], BF16, name="wg", tag="g", align_bytes=64)
+        copy_out("s", w_grouped, w_banks, 0)
+        copy_out("v", w_grouped, w_banks, 1)
+        copy_out("s", w_grouped, w_banks, 2)
+        copy_out("v", w_grouped, w_banks, 3)
+
+        nc.vector.tensor_copy(out=bzf[:], in_=bz[:])
+        b_bank = ps.tile([P, 512], F32, name="bb", tag="T")
+        nc.tensor.transpose(b_bank[:, 0:P], bzf[:], ident[:])
+        quantise(w_grouped, w_codes, w_planes)
+        nc.vector.tensor_copy(out=bias[:], in_=b_bank[:, 0:O_TILES])
+
+        mx_in = {}
+
+        def prepare(c, v_takes_last, n_before, n_after):
+            banks = transposes(x_tiles[c])
+            grouped = gp.tile([P, 4096], BF16, name="gr", tag="g", align_bytes=64)
+            codes = cp.tile([P, PASSES * CHUNK], U32, name="codes", tag="codes", align_bytes=64)
+            planes = cp.tile([P, PASSES * CHUNK], U8, name="planes", tag="planes", align_bytes=64)
+            copy_out("s", grouped, banks, 0)
+            copy_out("v", grouped, banks, 1)
+            copy_out("s", grouped, banks, 2)
+            copy_out("v" if v_takes_last else "s", grouped, banks, 3)
+            row_sums(n_before)
+            quantise(grouped, codes, planes)
+            row_sums(n_after)
+            mx_in[c] = (codes, planes)
+
+        vj_tiles = {}
+
+        def multiply(c):
+            codes, planes = mx_in[c]
+            vj = vjp.tile([P, O_TILES * CHUNK], F32, name="vj%d" % c)
+            vj_tiles[c] = vj
+            for ot in range(O_TILES):
+                z = ps.tile([P, CHUNK], F32, name="z", tag="Z")
+                for g in range(PASSES):
+                    nc.tensor.matmul_mx(
+                        out=z[:],
+                        lhsT=w_codes[:, g * OUTS + ot * P : g * OUTS + (ot + 1) * P].bitcast(FP8X4),
+                        lhsT_scale=w_planes[:, g * OUTS + ot * P : g * OUTS + (ot + 1) * P],
+                        rhs=codes[:, g * CHUNK : (g + 1) * CHUNK].bitcast(FP8X4),
+                        rhs_scale=planes[:, g * CHUNK : (g + 1) * CHUNK],
+                        start=(g == 0),
+                        stop=(g == PASSES - 1),
+                    )
+                nc.scalar.activation(
+                    out=vj[:, ot * CHUNK : (ot + 1) * CHUNK],
+                    in_=z[:],
+                    func=ACT.Relu,
+                    bias=bias[:, ot : ot + 1],
+                    scale=1.0,
+                    accum_out=acc[:, ot * N_CHUNKS + c : ot * N_CHUNKS + c + 1],
+                )
+
+        prepare(0, True, 0, 0)
+        for i in range(N_CHUNKS):
+            if i + X_BUFS - 1 < N_CHUNKS:
+                load(i + X_BUFS - 1)
+            if i + 1 < N_CHUNKS:
+                prepare(i + 1, i % 2 == 0, 1, ITEMS_PER_ITER - 1)
+            multiply(i)
+        row_sums(len(items))
+        nc.vector.tensor_scalar(
+            out=rsc_v[:, 0 : SUB * (N_CHUNKS - DEFERRED)],
+            in0=rs_v[:, 0 : SUB * (N_CHUNKS - DEFERRED)],
+            scalar1=C_HEBB,
+            scalar2=None,
+            op0=ALU.mult,
+        )
+
+        def back(c, t, tag):
+            bank = ps.tile([P, OUTS], F32, name="bk", tag=tag)
+            for ot in range(O_TILES):
+                nc.tensor.transpose(
+                    bank[:, ot * P : (ot + 1) * P],
+                    vj_tiles[c][:, ot * CHUNK + t * P : ot * CHUNK + (t + 1) * P],
+                    ident[:],
+                )
+            return bank
+
+        first = [back(0, t, "T") for t in range(SUB)]
+        nc.vector.tensor_reduce(
+            out=msum[:], in_=acc[:].rearrange("p (o c) -> p o c", o=O_TILES), axis=AX.X, op=ALU.add
+        )
+        nc.vector.tensor_scalar(out=mean[:], in0=msum[:], scalar1=1.0 / ROWS, scalar2=None, op0=ALU.mult)
+        m_bank = ps.tile([P, OUTS], F32, name="mbk", tag="Z")
+        for ot in range(O_TILES):
+            nc.tensor.matmul(
+                out=m_bank[:, ot * P : (ot + 1) * P],
+                lhsT=mean[:, ot : ot + 1].to_broadcast([P, P]),
+                rhs=ident[:],
+                start=True,
+                stop=True,
+            )
+        nc.vector.tensor_copy(out=mb[:], in_=m_bank[:])
+        nc.sync.dma_start(out=out_1.rearrange("(a o) -> a o", a=1), in_=mb[0:1, :])
+        for c in range(N_CHUNKS - DEFERRED, N_CHUNKS):
+            for t in range(SUB):
+                nc.scalar.activation(
+                    out=junk_s[:],
+                    in_=x_tiles[c][:, t * K_IN : (t + 1) * K_IN],
+                    func=ACT.Copy,
+                    scale=C_HEBB,
+                    accum_out=rsc_s[:, SUB * c + t : SUB * c + t + 1],
+                )
+
+        for c in range(N_CHUNKS):
+            if c % 2 == 0:
+                stage = gp.tile([P, SUB * OUTS], F32, name="stg", tag="g", align_bytes=64)
+            else:
+                stage = xp.tile([P, SUB * OUTS], F32, name="stx", tag="x")
+            rsc = rsc_v if c < N_CHUNKS - DEFERRED else rsc_s
+            for t in range(SUB):
+                bank = first[t] if c == 0 else back(c, t, "T" if c % 2 == 0 else "Z")
+                nc.vector.scalar_tensor_tensor(
+                    out=stage[:, t * OUTS : (t + 1) * OUTS],
+                    in0=mb[:],
+                    scalar=rsc[:, SUB * c + t : SUB * c + t + 1],
+                    in1=bank[:],
+                    op0=ALU.mult,
+                    op1=ALU.add,
+                )
+                if c == 0 or c == N_CHUNKS - 1:
+                    nc.sync.dma_start(out=out_ct[c, t], in_=stage[:, t * OUTS : (t + 1) * OUTS])
+            if 0 < c < N_CHUNKS - 1:
+                nc.sync.dma_start(out=out_c[c], in_=stage[:])

@@ -10,7 +10,6 @@ U8 = mybir.dt.uint8
 FP8X4 = mybir.dt.float8_e4m3fn_x4
 ALU = mybir.AluOpType
 ACT = mybir.ActivationFunctionType
-AX = mybir.AxisListType
 
 P = 128
 ROWS = 8192
@@ -25,7 +24,7 @@ C_HEBB = 0.01 * 0.001 / 1
 FLOPS = 2 * ROWS * K_IN * OUTS
 
 X_BUFS = 7
-DEFERRED = 5
+DEFERRED = 6
 ITEMS_PER_ITER = 3
 
 
@@ -39,7 +38,7 @@ def tile_optimalnet_pb_t_kernel(tc, vi, W, b, out_0, out_1):
 
     with ExitStack() as ctx:
         const = ctx.enter_context(tc.tile_pool(name="const", bufs=1))
-        vjp = ctx.enter_context(tc.tile_pool(name="vjp", bufs=1))
+        vjp = ctx.enter_context(tc.tile_pool(name="vjp", bufs=N_CHUNKS))
         xp = ctx.enter_context(tc.tile_pool(name="xp", bufs=X_BUFS))
         gp = ctx.enter_context(tc.tile_pool(name="gp", bufs=2))
         cp = ctx.enter_context(tc.tile_pool(name="cp", bufs=2))
@@ -51,7 +50,7 @@ def tile_optimalnet_pb_t_kernel(tc, vi, W, b, out_0, out_1):
         bzf = const.tile([P, P], F32, name="bzf")
         bias = const.tile([P, O_TILES], F32, name="bias")
         acc = const.tile([P, O_TILES * N_CHUNKS], F32, name="acc")
-        msum = const.tile([P, O_TILES], F32, name="msum")
+        junk_m = const.tile([P, N_CHUNKS], F32, name="junk_m")
         mean = const.tile([P, O_TILES], F32, name="mean")
         mb = const.tile([P, OUTS], F32, name="mb")
         rs_v = const.tile([P, N_CHUNKS * SUB], F32, name="rs_v")
@@ -95,17 +94,17 @@ def tile_optimalnet_pb_t_kernel(tc, vi, W, b, out_0, out_1):
                     banks.append(bank)
             return banks
 
-        def copy_out(engine, grouped, banks, j):
-            g32 = grouped[:].bitcast(F32)
-            dst = g32[:, 512 * j : 512 * j + 512].rearrange("p (c u) -> p c u", u=2)
-            src = banks[j][:].rearrange("p (u c) -> p c u", u=2)
+        def copy(engine, dst, src):
             if engine == "v":
                 nc.vector.tensor_copy(out=dst, in_=src)
             else:
                 nc.scalar.copy(out=dst, in_=src)
 
-        def quantise(grouped, codes, planes):
-            nc.vector.quantize_mx(out=codes[:].bitcast(FP8X4), scales=planes[:], in_=grouped[:])
+        def copy_out(engine, grouped, banks, j):
+            g32 = grouped[:].bitcast(F32)
+            dst = g32[:, 512 * j : 512 * j + 512].rearrange("p (c u) -> p c u", u=2)
+            src = banks[j][:].rearrange("p (u c) -> p c u", u=2)
+            copy(engine, dst, src)
 
         items = [(c, t) for c in range(N_CHUNKS - DEFERRED) for t in range(SUB)]
         taken = [0]
@@ -126,22 +125,37 @@ def tile_optimalnet_pb_t_kernel(tc, vi, W, b, out_0, out_1):
                     )
 
         wx = xp.tile([P, SUB * K_IN], BF16, name="wx", tag="x")
-        for t in range(O_TILES):
+        nc.sync.dma_start(out=wx[:, 0:K_IN], in_=w_t[0])
+        load(0)
+        for t in range(1, O_TILES):
             nc.sync.dma_start(out=wx[:, t * K_IN : (t + 1) * K_IN], in_=w_t[t])
-        for c in range(X_BUFS - 1):
+        for c in range(1, X_BUFS - 1):
             load(c)
-        w_banks = transposes(wx)
-        w_grouped = gp.tile([P, 4096], BF16, name="wg", tag="g", align_bytes=64)
-        copy_out("s", w_grouped, w_banks, 0)
-        copy_out("v", w_grouped, w_banks, 1)
-        copy_out("s", w_grouped, w_banks, 2)
-        copy_out("v", w_grouped, w_banks, 3)
 
-        nc.vector.tensor_copy(out=bzf[:], in_=bz[:])
-        b_bank = ps.tile([P, 512], F32, name="bb", tag="T")
-        nc.tensor.transpose(b_bank[:, 0:P], bzf[:], ident[:])
-        quantise(w_grouped, w_codes, w_planes)
-        nc.vector.tensor_copy(out=bias[:], in_=b_bank[:, 0:O_TILES])
+        w_grouped = gp.tile([P, 4096], BF16, name="wg", tag="g", align_bytes=64)
+        wx32 = wx[:].bitcast(F32)
+        wg32 = w_grouped[:].bitcast(F32)
+
+        def w_transposes(ot, engine):
+            bank = ps.tile([P, 512], F32, name="wb", tag="T")
+            for q in range(4):
+                nc.tensor.transpose(
+                    bank[:, 128 * q : 128 * q + 128],
+                    wx32[:, 512 * ot + 128 * q : 512 * ot + 128 * q + 128],
+                    ident[:],
+                )
+            copy(
+                engine,
+                wg32[:, 512 * ot : 512 * ot + 512].rearrange("p (g c u) -> p g c u", g=2, u=2),
+                bank[:].rearrange("p (g u c) -> p g c u", g=2, u=2),
+            )
+
+        def w_quantise(ot):
+            nc.vector.quantize_mx(
+                out=w_codes[:, 256 * ot : 256 * ot + 256].bitcast(FP8X4),
+                scales=w_planes[:, 256 * ot : 256 * ot + 256],
+                in_=w_grouped[:, 1024 * ot : 1024 * ot + 1024],
+            )
 
         mx_in = {}
 
@@ -155,7 +169,7 @@ def tile_optimalnet_pb_t_kernel(tc, vi, W, b, out_0, out_1):
             copy_out("s", grouped, banks, 2)
             copy_out("v" if v_takes_last else "s", grouped, banks, 3)
             row_sums(n_before)
-            quantise(grouped, codes, planes)
+            nc.vector.quantize_mx(out=codes[:].bitcast(FP8X4), scales=planes[:], in_=grouped[:])
             row_sums(n_after)
             mx_in[c] = (codes, planes)
 
@@ -163,15 +177,16 @@ def tile_optimalnet_pb_t_kernel(tc, vi, W, b, out_0, out_1):
 
         def multiply(c):
             codes, planes = mx_in[c]
-            vj = vjp.tile([P, O_TILES * CHUNK], F32, name="vj%d" % c)
+            vj = vjp.tile([P, O_TILES * CHUNK], F32, name="vj%d" % c, tag="vj")
             vj_tiles[c] = vj
             for ot in range(O_TILES):
                 z = ps.tile([P, CHUNK], F32, name="z", tag="Z")
                 for g in range(PASSES):
+                    w0 = 256 * ot + 128 * g
                     nc.tensor.matmul_mx(
                         out=z[:],
-                        lhsT=w_codes[:, g * OUTS + ot * P : g * OUTS + (ot + 1) * P].bitcast(FP8X4),
-                        lhsT_scale=w_planes[:, g * OUTS + ot * P : g * OUTS + (ot + 1) * P],
+                        lhsT=w_codes[:, w0 : w0 + P].bitcast(FP8X4),
+                        lhsT_scale=w_planes[:, w0 : w0 + P],
                         rhs=codes[:, g * CHUNK : (g + 1) * CHUNK].bitcast(FP8X4),
                         rhs_scale=planes[:, g * CHUNK : (g + 1) * CHUNK],
                         start=(g == 0),
@@ -185,38 +200,61 @@ def tile_optimalnet_pb_t_kernel(tc, vi, W, b, out_0, out_1):
                     scale=1.0,
                     accum_out=acc[:, ot * N_CHUNKS + c : ot * N_CHUNKS + c + 1],
                 )
+                if c == N_CHUNKS - 1:
+                    nc.vector.tensor_scalar(
+                        out=junk_m[:],
+                        in0=acc[:, ot * N_CHUNKS : (ot + 1) * N_CHUNKS],
+                        scalar1=1.0 / ROWS,
+                        scalar2=None,
+                        op0=ALU.mult,
+                        op1=ALU.add,
+                        accum_out=mean[:, ot : ot + 1],
+                    )
 
+        w_transposes(0, "s")
+        w_quantise(0)
+        nc.vector.tensor_copy(out=bzf[:], in_=bz[:])
         prepare(0, True, 0, 0)
-        for i in range(N_CHUNKS):
-            if i + X_BUFS - 1 < N_CHUNKS:
-                load(i + X_BUFS - 1)
+        w_transposes(1, "s")
+        w_transposes(2, "v")
+        w_transposes(3, "s")
+        b_bank = ps.tile([P, 512], F32, name="bb", tag="T")
+        nc.tensor.transpose(b_bank[:, 0:P], bzf[:], ident[:])
+        w_quantise(1)
+        w_quantise(2)
+        nc.vector.tensor_copy(out=bias[:], in_=b_bank[:, 0:O_TILES])
+        w_quantise(3)
+
+        multiply(0)
+        prepare(1, True, 1, ITEMS_PER_ITER - 1)
+        for i in range(1, N_CHUNKS):
+            if i + X_BUFS - 2 < N_CHUNKS:
+                load(i + X_BUFS - 2)
             if i + 1 < N_CHUNKS:
                 prepare(i + 1, i % 2 == 0, 1, ITEMS_PER_ITER - 1)
+            if i == N_CHUNKS - 1:
+                row_sums(len(items))
+                nc.vector.tensor_scalar(
+                    out=rsc_v[:, 0 : SUB * (N_CHUNKS - DEFERRED)],
+                    in0=rs_v[:, 0 : SUB * (N_CHUNKS - DEFERRED)],
+                    scalar1=C_HEBB,
+                    scalar2=None,
+                    op0=ALU.mult,
+                )
             multiply(i)
-        row_sums(len(items))
-        nc.vector.tensor_scalar(
-            out=rsc_v[:, 0 : SUB * (N_CHUNKS - DEFERRED)],
-            in0=rs_v[:, 0 : SUB * (N_CHUNKS - DEFERRED)],
-            scalar1=C_HEBB,
-            scalar2=None,
-            op0=ALU.mult,
-        )
 
         def back(c, t, tag):
             bank = ps.tile([P, OUTS], F32, name="bk", tag=tag)
             for ot in range(O_TILES):
-                nc.tensor.transpose(
-                    bank[:, ot * P : (ot + 1) * P],
-                    vj_tiles[c][:, ot * CHUNK + t * P : ot * CHUNK + (t + 1) * P],
-                    ident[:],
-                )
+                block = vj_tiles[c][:, ot * CHUNK + t * P : ot * CHUNK + (t + 1) * P]
+                if ot == 0 and (SUB * c + t) % 3 != 2:
+                    nc.tensor.matmul(out=bank[:, 0:P], lhsT=block, rhs=ident[:], start=True, stop=True)
+                else:
+                    nc.tensor.transpose(bank[:, ot * P : (ot + 1) * P], block, ident[:])
             return bank
 
         first = [back(0, t, "T") for t in range(SUB)]
-        nc.vector.tensor_reduce(
-            out=msum[:], in_=acc[:].rearrange("p (o c) -> p o c", o=O_TILES), axis=AX.X, op=ALU.add
-        )
-        nc.vector.tensor_scalar(out=mean[:], in0=msum[:], scalar1=1.0 / ROWS, scalar2=None, op0=ALU.mult)
+
         m_bank = ps.tile([P, OUTS], F32, name="mbk", tag="Z")
         for ot in range(O_TILES):
             nc.tensor.matmul(
@@ -227,7 +265,7 @@ def tile_optimalnet_pb_t_kernel(tc, vi, W, b, out_0, out_1):
                 stop=True,
             )
         nc.vector.tensor_copy(out=mb[:], in_=m_bank[:])
-        nc.sync.dma_start(out=out_1.rearrange("(a o) -> a o", a=1), in_=mb[0:1, :])
+        nc.gpsimd.dma_start(out=out_1.rearrange("(a o) -> a o", a=1), in_=mb[0:1, :])
         for c in range(N_CHUNKS - DEFERRED, N_CHUNKS):
             for t in range(SUB):
                 nc.scalar.activation(
@@ -239,10 +277,10 @@ def tile_optimalnet_pb_t_kernel(tc, vi, W, b, out_0, out_1):
                 )
 
         for c in range(N_CHUNKS):
-            if c % 2 == 0:
+            if c < 2:
                 stage = gp.tile([P, SUB * OUTS], F32, name="stg", tag="g", align_bytes=64)
             else:
-                stage = xp.tile([P, SUB * OUTS], F32, name="stx", tag="x")
+                stage = vjp.tile([P, SUB * OUTS], F32, name="stv", tag="vj")
             rsc = rsc_v if c < N_CHUNKS - DEFERRED else rsc_s
             for t in range(SUB):
                 bank = first[t] if c == 0 else back(c, t, "T" if c % 2 == 0 else "Z")

@@ -56,8 +56,6 @@ def tile_optimalnet_pb_t_kernel(tc, vi, W, b, out_0, out_1):
         rs_v = const.tile([P, N_CHUNKS * SUB], F32, name="rs_v")
         rsc_v = const.tile([P, N_CHUNKS * SUB], F32, name="rsc_v")
         rsc_s = const.tile([P, N_CHUNKS * SUB], F32, name="rsc_s")
-        junk_v = const.tile([P, K_IN], BF16, name="junk_v")
-        junk_s = const.tile([P, K_IN], BF16, name="junk_s")
         w_codes = const.tile([P, PASSES * OUTS], U32, name="w_codes", align_bytes=64)
         w_planes = const.tile([P, PASSES * OUTS], U8, name="w_planes", align_bytes=64)
 
@@ -115,7 +113,7 @@ def tile_optimalnet_pb_t_kernel(tc, vi, W, b, out_0, out_1):
                     c, t = items[taken[0]]
                     taken[0] = taken[0] + 1
                     nc.vector.tensor_scalar(
-                        out=junk_v[:],
+                        out=x_tiles[c][:, t * K_IN : (t + 1) * K_IN],
                         in0=x_tiles[c][:, t * K_IN : (t + 1) * K_IN],
                         scalar1=1.0,
                         scalar2=None,
@@ -269,7 +267,7 @@ def tile_optimalnet_pb_t_kernel(tc, vi, W, b, out_0, out_1):
         for c in range(N_CHUNKS - DEFERRED, N_CHUNKS):
             for t in range(SUB):
                 nc.scalar.activation(
-                    out=junk_s[:],
+                    out=x_tiles[c][:, t * K_IN : (t + 1) * K_IN],
                     in_=x_tiles[c][:, t * K_IN : (t + 1) * K_IN],
                     func=ACT.Copy,
                     scale=C_HEBB,

@@ -251,18 +251,21 @@ def tile_optimalnet_pb_t_kernel(tc, vi, W, b, out_0, out_1):
                     nc.tensor.transpose(bank[:, ot * P : (ot + 1) * P], block, ident[:])
             return bank
 
-        first = [back(0, t, "T") for t in range(SUB)]
+        first = [back(0, 0, "T")]
 
-        m_bank = ps.tile([P, OUTS], F32, name="mbk", tag="Z")
+        m_banks = [ps.tile([P, OUTS], F32, name="mbk%d" % h, tag="Z") for h in range(2)]
         for ot in range(O_TILES):
             nc.tensor.matmul(
-                out=m_bank[:, ot * P : (ot + 1) * P],
+                out=m_banks[ot // 2][:, (ot % 2) * P : (ot % 2 + 1) * P],
                 lhsT=mean[:, ot : ot + 1].to_broadcast([P, P]),
                 rhs=ident[:],
                 start=True,
                 stop=True,
             )
-        nc.vector.tensor_copy(out=mb[:], in_=m_bank[:])
+        nc.vector.tensor_copy(out=mb[:, 0 : 2 * P], in_=m_banks[0][:, 0 : 2 * P])
+        nc.scalar.copy(out=mb[:, 2 * P : 4 * P], in_=m_banks[1][:, 0 : 2 * P])
+        for t in range(1, SUB):
+            first.append(back(0, t, "T"))
         nc.gpsimd.dma_start(out=out_1.rearrange("(a o) -> a o", a=1), in_=mb[0:1, :])
         for c in range(N_CHUNKS - DEFERRED, N_CHUNKS):
             for t in range(SUB):
@@ -292,5 +295,8 @@ def tile_optimalnet_pb_t_kernel(tc, vi, W, b, out_0, out_1):
                 )
                 if c == 0 or c == N_CHUNKS - 1:
                     nc.sync.dma_start(out=out_ct[c, t], in_=stage[:, t * OUTS : (t + 1) * OUTS])
-            if 0 < c < N_CHUNKS - 1:
-                nc.sync.dma_start(out=out_c[c], in_=stage[:])
+                elif t % 2 == 1:
+                    nc.sync.dma_start(
+                        out=out_c[c][:, (t - 1) * OUTS : (t + 1) * OUTS],
+                        in_=stage[:, (t - 1) * OUTS : (t + 1) * OUTS],
+                    )

@@ -245,10 +245,7 @@ def tile_optimalnet_pb_t_kernel(tc, vi, W, b, out_0, out_1):
             bank = ps.tile([P, OUTS], F32, name="bk", tag=tag)
             for ot in range(O_TILES):
                 block = vj_tiles[c][:, ot * CHUNK + t * P : ot * CHUNK + (t + 1) * P]
-                if ot == 0 and (SUB * c + t) % 3 != 2:
-                    nc.tensor.matmul(out=bank[:, 0:P], lhsT=block, rhs=ident[:], start=True, stop=True)
-                else:
-                    nc.tensor.transpose(bank[:, ot * P : (ot + 1) * P], block, ident[:])
+                nc.tensor.transpose(bank[:, ot * P : (ot + 1) * P], block, ident[:])
             return bank
 
         first = [back(0, 0, "T")]

@@ -23,9 +23,9 @@ PASSES = K_IN // 512
 C_HEBB = 0.01 * 0.001 / 1
 FLOPS = 2 * ROWS * K_IN * OUTS
 
-X_BUFS = 7
-DEFERRED = 6
-ITEMS_PER_ITER = 3
+DEFERRED = 7
+ON_VECTOR = N_CHUNKS - DEFERRED
+SLOT_BYTES = 8192
 
 
 def tile_optimalnet_pb_t_kernel(tc, vi, W, b, out_0, out_1):
@@ -38,8 +38,7 @@ def tile_optimalnet_pb_t_kernel(tc, vi, W, b, out_0, out_1):
 
     with ExitStack() as ctx:
         const = ctx.enter_context(tc.tile_pool(name="const", bufs=1))
-        vjp = ctx.enter_context(tc.tile_pool(name="vjp", bufs=N_CHUNKS))
-        xp = ctx.enter_context(tc.tile_pool(name="xp", bufs=X_BUFS))
+        slots = ctx.enter_context(tc.tile_pool(name="slots", bufs=1))
         gp = ctx.enter_context(tc.tile_pool(name="gp", bufs=2))
         cp = ctx.enter_context(tc.tile_pool(name="cp", bufs=2))
         ps = ctx.enter_context(tc.psum_pool(name="ps", bufs=4))
@@ -51,7 +50,9 @@ def tile_optimalnet_pb_t_kernel(tc, vi, W, b, out_0, out_1):
         bias = const.tile([P, O_TILES], F32, name="bias")
         acc = const.tile([P, O_TILES * N_CHUNKS], F32, name="acc")
         junk_m = const.tile([P, N_CHUNKS], F32, name="junk_m")
-        mean = const.tile([P, O_TILES], F32, name="mean")
+        part = const.tile([P, O_TILES], F32, name="part")
+        zeros = const.tile([P, CHUNK], F32, name="zeros")
+        ident_mean = const.tile([P, P], F32, name="ident_mean")
         mb = const.tile([P, OUTS], F32, name="mb")
         rs_v = const.tile([P, N_CHUNKS * SUB], F32, name="rs_v")
         rsc_v = const.tile([P, N_CHUNKS * SUB], F32, name="rsc_v")
@@ -60,13 +61,27 @@ def tile_optimalnet_pb_t_kernel(tc, vi, W, b, out_0, out_1):
         w_planes = const.tile([P, PASSES * OUTS], U8, name="w_planes", align_bytes=64)
 
         make_identity(nc, ident[:])
+        nc.gpsimd.memset(zeros[:], 0.0)
         nc.vector.memset(bz[:], 0.0)
+        nc.vector.tensor_scalar(
+            out=ident_mean[:], in0=ident[:], scalar1=1.0 / ROWS, scalar2=None, op0=ALU.mult
+        )
         nc.scalar.dma_start(out=bz[0:O_TILES, :], in_=b.rearrange("(t p) -> t p", p=P))
+
+        def x_slot(c):
+            return c - ON_VECTOR if c >= ON_VECTOR else DEFERRED + 1 + c
+
+        def vj_slot(c):
+            own = N_CHUNKS - ON_VECTOR - 1
+            return N_CHUNKS + 1 + c if c < own else DEFERRED + c - own
+
+        def in_slot(slot, dtype, name):
+            return slots.tile([P, SLOT_BYTES // (2 if dtype == BF16 else 4)], dtype, name=name, tag="slot%d" % slot)
 
         x_tiles = {}
 
         def load(c):
-            x = xp.tile([P, SUB * K_IN], BF16, name="x%d" % c, tag="x")
+            x = in_slot(x_slot(c), BF16, "x%d" % c)
             x_tiles[c] = x
             if c == 0:
                 for t in range(SUB):
@@ -76,9 +91,9 @@ def tile_optimalnet_pb_t_kernel(tc, vi, W, b, out_0, out_1):
 
         def transposes(x):
             x32 = x[:].bitcast(F32)
-            banks = []
-            for g in range(PASSES):
-                for tp in range(2):
+            banks = {}
+            for tp in range(2):
+                for g in range(PASSES):
                     bank = ps.tile([P, 512], F32, name="tb", tag="T")
                     for tt in range(2):
                         t = 2 * tp + tt
@@ -89,7 +104,7 @@ def tile_optimalnet_pb_t_kernel(tc, vi, W, b, out_0, out_1):
                                 x32[:, col : col + 128],
                                 ident[:],
                             )
-                    banks.append(bank)
+                    banks[2 * g + tp] = bank
             return banks
 
         def copy(engine, dst, src):
@@ -104,7 +119,7 @@ def tile_optimalnet_pb_t_kernel(tc, vi, W, b, out_0, out_1):
             src = banks[j][:].rearrange("p (u c) -> p c u", u=2)
             copy(engine, dst, src)
 
-        items = [(c, t) for c in range(N_CHUNKS - DEFERRED) for t in range(SUB)]
+        items = [(c, t) for c in range(ON_VECTOR) for t in range(SUB)]
         taken = [0]
 
         def row_sums(n):
@@ -122,12 +137,12 @@ def tile_optimalnet_pb_t_kernel(tc, vi, W, b, out_0, out_1):
                         accum_out=rs_v[:, SUB * c + t : SUB * c + t + 1],
                     )
 
-        wx = xp.tile([P, SUB * K_IN], BF16, name="wx", tag="x")
+        wx = in_slot(DEFERRED, BF16, "wx")
         nc.sync.dma_start(out=wx[:, 0:K_IN], in_=w_t[0])
         load(0)
         for t in range(1, O_TILES):
             nc.sync.dma_start(out=wx[:, t * K_IN : (t + 1) * K_IN], in_=w_t[t])
-        for c in range(1, X_BUFS - 1):
+        for c in range(1, N_CHUNKS):
             load(c)
 
         w_grouped = gp.tile([P, 4096], BF16, name="wg", tag="g", align_bytes=64)
@@ -135,7 +150,7 @@ def tile_optimalnet_pb_t_kernel(tc, vi, W, b, out_0, out_1):
         wg32 = w_grouped[:].bitcast(F32)
 
         def w_transposes(ot, engine):
-            bank = ps.tile([P, 512], F32, name="wb", tag="T")
+            bank = ps.tile([P, 512], F32, name="wb", tag="Z")
             for q in range(4):
                 nc.tensor.transpose(
                     bank[:, 128 * q : 128 * q + 128],
@@ -157,84 +172,113 @@ def tile_optimalnet_pb_t_kernel(tc, vi, W, b, out_0, out_1):
 
         mx_in = {}
 
-        def prepare(c, v_takes_last, n_before, n_after):
+        def prepare(c):
+            due = len(items) * c // (N_CHUNKS - 1) - taken[0]
             banks = transposes(x_tiles[c])
             grouped = gp.tile([P, 4096], BF16, name="gr", tag="g", align_bytes=64)
             codes = cp.tile([P, PASSES * CHUNK], U32, name="codes", tag="codes", align_bytes=64)
             planes = cp.tile([P, PASSES * CHUNK], U8, name="planes", tag="planes", align_bytes=64)
-            copy_out("s", grouped, banks, 0)
-            copy_out("v", grouped, banks, 1)
+            copy_out("v", grouped, banks, 0)
             copy_out("s", grouped, banks, 2)
-            copy_out("v" if v_takes_last else "s", grouped, banks, 3)
-            row_sums(n_before)
-            nc.vector.quantize_mx(out=codes[:].bitcast(FP8X4), scales=planes[:], in_=grouped[:])
-            row_sums(n_after)
+            copy_out("v", grouped, banks, 1)
+            copy_out("s", grouped, banks, 3)
+            row_sums(due // 2)
+            if c < 2:
+                for g in range(PASSES):
+                    cols = slice(g * CHUNK, (g + 1) * CHUNK)
+                    nc.vector.quantize_mx(
+                        out=codes[:, cols].bitcast(FP8X4),
+                        scales=planes[:, cols],
+                        in_=grouped[:, 4 * g * CHUNK : 4 * (g + 1) * CHUNK],
+                    )
+            else:
+                nc.vector.quantize_mx(out=codes[:].bitcast(FP8X4), scales=planes[:], in_=grouped[:])
+            row_sums(due - due // 2)
             mx_in[c] = (codes, planes)
 
         vj_tiles = {}
 
         def multiply(c):
             codes, planes = mx_in[c]
-            vj = vjp.tile([P, O_TILES * CHUNK], F32, name="vj%d" % c, tag="vj")
+            vj = in_slot(vj_slot(c), F32, "vj%d" % c)
             vj_tiles[c] = vj
-            for ot in range(O_TILES):
-                z = ps.tile([P, CHUNK], F32, name="z", tag="Z")
-                for g in range(PASSES):
-                    w0 = 256 * ot + 128 * g
-                    nc.tensor.matmul_mx(
-                        out=z[:],
-                        lhsT=w_codes[:, w0 : w0 + P].bitcast(FP8X4),
-                        lhsT_scale=w_planes[:, w0 : w0 + P],
-                        rhs=codes[:, g * CHUNK : (g + 1) * CHUNK].bitcast(FP8X4),
-                        rhs_scale=planes[:, g * CHUNK : (g + 1) * CHUNK],
-                        start=(g == 0),
-                        stop=(g == PASSES - 1),
-                    )
-                nc.scalar.activation(
-                    out=vj[:, ot * CHUNK : (ot + 1) * CHUNK],
-                    in_=z[:],
-                    func=ACT.Relu,
-                    bias=bias[:, ot : ot + 1],
-                    scale=1.0,
-                    accum_out=acc[:, ot * N_CHUNKS + c : ot * N_CHUNKS + c + 1],
+            z_banks = {}
+
+            def mx_pass(ot, g):
+                if g == 0:
+                    z_banks[ot] = ps.tile([P, CHUNK], F32, name="z", tag="Z")
+                w0 = 256 * ot + 128 * g
+                nc.tensor.matmul_mx(
+                    out=z_banks[ot][:],
+                    lhsT=w_codes[:, w0 : w0 + P].bitcast(FP8X4),
+                    lhsT_scale=w_planes[:, w0 : w0 + P],
+                    rhs=codes[:, g * CHUNK : (g + 1) * CHUNK].bitcast(FP8X4),
+                    rhs_scale=planes[:, g * CHUNK : (g + 1) * CHUNK],
+                    start=(g == 0),
+                    stop=(g == PASSES - 1),
                 )
-                if c == N_CHUNKS - 1:
+
+            for ot in range(O_TILES):
+                if c == 1 and ot < 2:
+                    if ot == 0:
+                        mx_pass(0, 0)
+                        mx_pass(1, 0)
+                    mx_pass(ot, 1)
+                else:
+                    for g in range(PASSES):
+                        mx_pass(ot, g)
+                if c == N_CHUNKS - 1 and ot % 2 == 1:
+                    nc.vector.scalar_tensor_tensor(
+                        out=vj[:, ot * CHUNK : (ot + 1) * CHUNK],
+                        in0=z_banks[ot][:],
+                        scalar=bias[:, ot : ot + 1],
+                        in1=zeros[:],
+                        op0=ALU.add,
+                        op1=ALU.max,
+                        accum_out=acc[:, ot * N_CHUNKS + c : ot * N_CHUNKS + c + 1],
+                    )
+                else:
+                    nc.scalar.activation(
+                        out=vj[:, ot * CHUNK : (ot + 1) * CHUNK],
+                        in_=z_banks[ot][:],
+                        func=ACT.Relu,
+                        bias=bias[:, ot : ot + 1],
+                        scale=1.0,
+                        accum_out=acc[:, ot * N_CHUNKS + c : ot * N_CHUNKS + c + 1],
+                    )
+                if c == N_CHUNKS - 2:
                     nc.vector.tensor_scalar(
-                        out=junk_m[:],
-                        in0=acc[:, ot * N_CHUNKS : (ot + 1) * N_CHUNKS],
-                        scalar1=1.0 / ROWS,
+                        out=junk_m[:, 0 : N_CHUNKS - 1],
+                        in0=acc[:, ot * N_CHUNKS : (ot + 1) * N_CHUNKS - 1],
+                        scalar1=1.0,
                         scalar2=None,
                         op0=ALU.mult,
                         op1=ALU.add,
-                        accum_out=mean[:, ot : ot + 1],
+                        accum_out=part[:, ot : ot + 1],
                     )
 
         w_transposes(0, "s")
         w_quantise(0)
         nc.vector.tensor_copy(out=bzf[:], in_=bz[:])
-        prepare(0, True, 0, 0)
-        w_transposes(1, "s")
-        w_transposes(2, "v")
-        w_transposes(3, "s")
+        prepare(0)
+        for ot in range(1, O_TILES):
+            w_transposes(ot, "s")
         b_bank = ps.tile([P, 512], F32, name="bb", tag="T")
         nc.tensor.transpose(b_bank[:, 0:P], bzf[:], ident[:])
         w_quantise(1)
-        w_quantise(2)
         nc.vector.tensor_copy(out=bias[:], in_=b_bank[:, 0:O_TILES])
+        w_quantise(2)
         w_quantise(3)
 
         multiply(0)
-        prepare(1, True, 1, ITEMS_PER_ITER - 1)
+        prepare(1)
         for i in range(1, N_CHUNKS):
-            if i + X_BUFS - 2 < N_CHUNKS:
-                load(i + X_BUFS - 2)
             if i + 1 < N_CHUNKS:
-                prepare(i + 1, i % 2 == 0, 1, ITEMS_PER_ITER - 1)
+                prepare(i + 1)
             if i == N_CHUNKS - 1:
-                row_sums(len(items))
                 nc.vector.tensor_scalar(
-                    out=rsc_v[:, 0 : SUB * (N_CHUNKS - DEFERRED)],
-                    in0=rs_v[:, 0 : SUB * (N_CHUNKS - DEFERRED)],
+                    out=rsc_v[:, 0 : SUB * ON_VECTOR],
+                    in0=rs_v[:, 0 : SUB * ON_VECTOR],
                     scalar1=C_HEBB,
                     scalar2=None,
                     op0=ALU.mult,
@@ -250,21 +294,25 @@ def tile_optimalnet_pb_t_kernel(tc, vi, W, b, out_0, out_1):
 
         first = [back(0, 0, "T")]
 
-        m_banks = [ps.tile([P, OUTS], F32, name="mbk%d" % h, tag="Z") for h in range(2)]
+        m_bank = ps.tile([P, OUTS], F32, name="mbk", tag="Z")
+        m_bank_last = ps.tile([P, OUTS], F32, name="mbl", tag="Z")
+        last = O_TILES - 1
         for ot in range(O_TILES):
-            nc.tensor.matmul(
-                out=m_banks[ot // 2][:, (ot % 2) * P : (ot % 2 + 1) * P],
-                lhsT=mean[:, ot : ot + 1].to_broadcast([P, P]),
-                rhs=ident[:],
-                start=True,
-                stop=True,
-            )
-        nc.vector.tensor_copy(out=mb[:, 0 : 2 * P], in_=m_banks[0][:, 0 : 2 * P])
-        nc.scalar.copy(out=mb[:, 2 * P : 4 * P], in_=m_banks[1][:, 0 : 2 * P])
+            sums = [part[:, ot : ot + 1], acc[:, (ot + 1) * N_CHUNKS - 1 : (ot + 1) * N_CHUNKS]]
+            for h in range(2):
+                nc.tensor.matmul(
+                    out=(m_bank_last if ot == last else m_bank)[:, ot * P : (ot + 1) * P],
+                    lhsT=sums[h].to_broadcast([P, P]),
+                    rhs=ident_mean[:],
+                    start=(h == 0),
+                    stop=(h == 1),
+                )
+        nc.vector.tensor_copy(out=mb[:, 0 : last * P], in_=m_bank[:, 0 : last * P])
+        nc.scalar.copy(out=mb[:, last * P : OUTS], in_=m_bank_last[:, last * P : OUTS])
         for t in range(1, SUB):
             first.append(back(0, t, "T"))
         nc.gpsimd.dma_start(out=out_1.rearrange("(a o) -> a o", a=1), in_=mb[0:1, :])
-        for c in range(N_CHUNKS - DEFERRED, N_CHUNKS):
+        for c in range(ON_VECTOR, N_CHUNKS):
             for t in range(SUB):
                 nc.scalar.activation(
                     out=x_tiles[c][:, t * K_IN : (t + 1) * K_IN],
@@ -278,8 +326,8 @@ def tile_optimalnet_pb_t_kernel(tc, vi, W, b, out_0, out_1):
             if c < 2:
                 stage = gp.tile([P, SUB * OUTS], F32, name="stg", tag="g", align_bytes=64)
             else:
-                stage = vjp.tile([P, SUB * OUTS], F32, name="stv", tag="vj")
-            rsc = rsc_v if c < N_CHUNKS - DEFERRED else rsc_s
+                stage = in_slot(vj_slot(c - 2), F32, "st%d" % c)
+            rsc = rsc_v if c < ON_VECTOR else rsc_s
             for t in range(SUB):
                 bank = first[t] if c == 0 else back(c, t, "T" if c % 2 == 0 else "Z")
                 nc.vector.scalar_tensor_tensor(

@@ -23,7 +23,7 @@ PASSES = K_IN // 512
 C_HEBB = 0.01 * 0.001 / 1
 FLOPS = 2 * ROWS * K_IN * OUTS
 
-DEFERRED = 7
+DEFERRED = 9
 ON_VECTOR = N_CHUNKS - DEFERRED
 SLOT_BYTES = 8192
 
@@ -39,7 +39,6 @@ def tile_optimalnet_pb_t_kernel(tc, vi, W, b, out_0, out_1):
     with ExitStack() as ctx:
         const = ctx.enter_context(tc.tile_pool(name="const", bufs=1))
         slots = ctx.enter_context(tc.tile_pool(name="slots", bufs=1))
-        gp = ctx.enter_context(tc.tile_pool(name="gp", bufs=2))
         cp = ctx.enter_context(tc.tile_pool(name="cp", bufs=2))
         ps = ctx.enter_context(tc.psum_pool(name="ps", bufs=4))
         ctx.enter_context(tc.manual_schedule())
@@ -51,7 +50,6 @@ def tile_optimalnet_pb_t_kernel(tc, vi, W, b, out_0, out_1):
         acc = const.tile([P, O_TILES * N_CHUNKS], F32, name="acc")
         junk_m = const.tile([P, N_CHUNKS], F32, name="junk_m")
         part = const.tile([P, O_TILES], F32, name="part")
-        zeros = const.tile([P, CHUNK], F32, name="zeros")
         ident_mean = const.tile([P, P], F32, name="ident_mean")
         mb = const.tile([P, OUTS], F32, name="mb")
         rs_v = const.tile([P, N_CHUNKS * SUB], F32, name="rs_v")
@@ -61,22 +59,32 @@ def tile_optimalnet_pb_t_kernel(tc, vi, W, b, out_0, out_1):
         w_planes = const.tile([P, PASSES * OUTS], U8, name="w_planes", align_bytes=64)
 
         make_identity(nc, ident[:])
-        nc.gpsimd.memset(zeros[:], 0.0)
+        nc.gpsimd.memset(mb[:], 0.0)
         nc.vector.memset(bz[:], 0.0)
         nc.vector.tensor_scalar(
             out=ident_mean[:], in0=ident[:], scalar1=1.0 / ROWS, scalar2=None, op0=ALU.mult
         )
         nc.scalar.dma_start(out=bz[0:O_TILES, :], in_=b.rearrange("(t p) -> t p", p=P))
 
+        own = N_CHUNKS - 2 - (ON_VECTOR - 1)
+
         def x_slot(c):
             return c - ON_VECTOR if c >= ON_VECTOR else DEFERRED + 1 + c
 
+        def grouped_slot(c):
+            return N_CHUNKS + 1 + c % 2
+
         def vj_slot(c):
-            own = N_CHUNKS - ON_VECTOR - 1
-            return N_CHUNKS + 1 + c if c < own else DEFERRED + c - own
+            if c >= N_CHUNKS - 2:
+                return grouped_slot(c)
+            return N_CHUNKS + 3 + c if c < own else x_slot(c - own)
+
+        def out_slot(c):
+            return (DEFERRED, x_slot(ON_VECTOR - 1))[c] if c < 2 else vj_slot(c - 2)
 
         def in_slot(slot, dtype, name):
-            return slots.tile([P, SLOT_BYTES // (2 if dtype == BF16 else 4)], dtype, name=name, tag="slot%d" % slot)
+            width = SLOT_BYTES // (2 if dtype == BF16 else 4)
+            return slots.tile([P, width], dtype, name=name, tag="slot%d" % slot, align_bytes=64)
 
         x_tiles = {}
 
@@ -145,7 +153,7 @@ def tile_optimalnet_pb_t_kernel(tc, vi, W, b, out_0, out_1):
         for c in range(1, N_CHUNKS):
             load(c)
 
-        w_grouped = gp.tile([P, 4096], BF16, name="wg", tag="g", align_bytes=64)
+        w_grouped = in_slot(grouped_slot(1), BF16, "wg")
         wx32 = wx[:].bitcast(F32)
         wg32 = w_grouped[:].bitcast(F32)
 
@@ -173,9 +181,9 @@ def tile_optimalnet_pb_t_kernel(tc, vi, W, b, out_0, out_1):
         mx_in = {}
 
         def prepare(c):
-            due = len(items) * c // (N_CHUNKS - 1) - taken[0]
+            due = min(len(items), len(items) * c // (N_CHUNKS - 2)) - taken[0]
             banks = transposes(x_tiles[c])
-            grouped = gp.tile([P, 4096], BF16, name="gr", tag="g", align_bytes=64)
+            grouped = in_slot(grouped_slot(c), BF16, "gr%d" % c)
             codes = cp.tile([P, PASSES * CHUNK], U32, name="codes", tag="codes", align_bytes=64)
             planes = cp.tile([P, PASSES * CHUNK], U8, name="planes", tag="planes", align_bytes=64)
             copy_out("v", grouped, banks, 0)
@@ -232,7 +240,7 @@ def tile_optimalnet_pb_t_kernel(tc, vi, W, b, out_0, out_1):
                         out=vj[:, ot * CHUNK : (ot + 1) * CHUNK],
                         in0=z_banks[ot][:],
                         scalar=bias[:, ot : ot + 1],
-                        in1=zeros[:],
+                        in1=mb[:],
                         op0=ALU.add,
                         op1=ALU.max,
                         accum_out=acc[:, ot * N_CHUNKS + c : ot * N_CHUNKS + c + 1],
@@ -308,25 +316,30 @@ def tile_optimalnet_pb_t_kernel(tc, vi, W, b, out_0, out_1):
                     stop=(h == 1),
                 )
         nc.vector.tensor_copy(out=mb[:, 0 : last * P], in_=m_bank[:, 0 : last * P])
-        nc.scalar.copy(out=mb[:, last * P : OUTS], in_=m_bank_last[:, last * P : OUTS])
+        nc.vector.tensor_copy(out=mb[:, last * P : OUTS], in_=m_bank_last[:, last * P : OUTS])
         for t in range(1, SUB):
             first.append(back(0, t, "T"))
-        nc.gpsimd.dma_start(out=out_1.rearrange("(a o) -> a o", a=1), in_=mb[0:1, :])
+
         for c in range(ON_VECTOR, N_CHUNKS):
             for t in range(SUB):
+                x_row = x_tiles[c][:, t * K_IN : (t + 1) * K_IN]
+                if t % 2 == 1:
+                    half = cp.tile([P, K_IN // 2], F32, name="half", tag="codes", align_bytes=64)
+                    nc.gpsimd.tensor_tensor(
+                        out=half[:], in0=x_row[:, 0 : K_IN // 2], in1=x_row[:, K_IN // 2 : K_IN], op=ALU.add
+                    )
+                    x_row = half[:]
                 nc.scalar.activation(
-                    out=x_tiles[c][:, t * K_IN : (t + 1) * K_IN],
-                    in_=x_tiles[c][:, t * K_IN : (t + 1) * K_IN],
+                    out=x_row,
+                    in_=x_row,
                     func=ACT.Copy,
                     scale=C_HEBB,
                     accum_out=rsc_s[:, SUB * c + t : SUB * c + t + 1],
                 )
+        nc.gpsimd.dma_start(out=out_1.rearrange("(a o) -> a o", a=1), in_=mb[0:1, :])
 
         for c in range(N_CHUNKS):
-            if c < 2:
-                stage = gp.tile([P, SUB * OUTS], F32, name="stg", tag="g", align_bytes=64)
-            else:
-                stage = in_slot(vj_slot(c - 2), F32, "st%d" % c)
+            stage = in_slot(out_slot(c), F32, "st%d" % c)
             rsc = rsc_v if c < ON_VECTOR else rsc_s
             for t in range(SUB):
                 bank = first[t] if c == 0 else back(c, t, "T" if c % 2 == 0 else "Z")

@@ -23,6 +23,7 @@ PASSES = K_IN // 512
 C_HEBB = 0.01 * 0.001 / 1
 FLOPS = 2 * ROWS * K_IN * OUTS
 
+EARLY_SUMS = 2
 DEFERRED = 9
 ON_VECTOR = N_CHUNKS - DEFERRED
 SLOT_BYTES = 8192
@@ -77,10 +78,10 @@ def tile_optimalnet_pb_t_kernel(tc, vi, W, b, out_0, out_1):
         def vj_slot(c):
             if c >= N_CHUNKS - 2:
                 return grouped_slot(c)
-            return N_CHUNKS + 3 + c if c < own else x_slot(c - own)
+            return N_CHUNKS + 3 + c if c < own else DEFERRED + c - own
 
         def out_slot(c):
-            return (DEFERRED, x_slot(ON_VECTOR - 1))[c] if c < 2 else vj_slot(c - 2)
+            return x_slot(ON_VECTOR - 2 + c) if c < 2 else vj_slot(c - 2)
 
         def in_slot(slot, dtype, name):
             width = SLOT_BYTES // (2 if dtype == BF16 else 4)
@@ -181,7 +182,7 @@ def tile_optimalnet_pb_t_kernel(tc, vi, W, b, out_0, out_1):
         mx_in = {}
 
         def prepare(c):
-            due = min(len(items), len(items) * c // (N_CHUNKS - 2)) - taken[0]
+            due = EARLY_SUMS + 3 * (c - 1) // 2 - taken[0] if c > 1 else 0
             banks = transposes(x_tiles[c])
             grouped = in_slot(grouped_slot(c), BF16, "gr%d" % c)
             codes = cp.tile([P, PASSES * CHUNK], U32, name="codes", tag="codes", align_bytes=64)
@@ -277,6 +278,7 @@ def tile_optimalnet_pb_t_kernel(tc, vi, W, b, out_0, out_1):
         nc.vector.tensor_copy(out=bias[:], in_=b_bank[:, 0:O_TILES])
         w_quantise(2)
         w_quantise(3)
+        row_sums(EARLY_SUMS)
 
         multiply(0)
         prepare(1)
@@ -284,6 +286,7 @@ def tile_optimalnet_pb_t_kernel(tc, vi, W, b, out_0, out_1):
             if i + 1 < N_CHUNKS:
                 prepare(i + 1)
             if i == N_CHUNKS - 1:
+                row_sums(len(items))
                 nc.vector.tensor_scalar(
                     out=rsc_v[:, 0 : SUB * ON_VECTOR],
                     in0=rs_v[:, 0 : SUB * ON_VECTOR],

@@ -23,6 +23,7 @@ PASSES = K_IN // 512
 C_HEBB = 0.01 * 0.001 / 1
 FLOPS = 2 * ROWS * K_IN * OUTS
 
+WARM_UP = 4
 EARLY_SUMS = 2
 DEFERRED = 9
 ON_VECTOR = N_CHUNKS - DEFERRED
@@ -46,10 +47,11 @@ def tile_optimalnet_pb_t_kernel(tc, vi, W, b, out_0, out_1):
 
         ident = const.tile([P, P], F32, name="ident")
         bz = const.tile([P, P], BF16, name="bz")
+        bb16 = const.tile([P, P], BF16, name="bb16")
         bzf = const.tile([P, P], F32, name="bzf")
         bias = const.tile([P, O_TILES], F32, name="bias")
         acc = const.tile([P, O_TILES * N_CHUNKS], F32, name="acc")
-        junk_m = const.tile([P, N_CHUNKS], F32, name="junk_m")
+        idle = const.tile([P, OUTS], BF16, name="idle")
         part = const.tile([P, O_TILES], F32, name="part")
         ident_mean = const.tile([P, P], F32, name="ident_mean")
         mb = const.tile([P, OUTS], F32, name="mb")
@@ -61,11 +63,17 @@ def tile_optimalnet_pb_t_kernel(tc, vi, W, b, out_0, out_1):
 
         make_identity(nc, ident[:])
         nc.gpsimd.memset(mb[:], 0.0)
+        nc.vector.memset(bb16[:], 0.0)
         nc.vector.memset(bz[:], 0.0)
+        nc.vector.memset(idle[:], 0.0)
+
+        def keep_clock(bank):
+            nc.tensor.matmul(out=bank[:], lhsT=bz[:], rhs=idle[:], start=True, stop=True)
+
         nc.vector.tensor_scalar(
             out=ident_mean[:], in0=ident[:], scalar1=1.0 / ROWS, scalar2=None, op0=ALU.mult
         )
-        nc.scalar.dma_start(out=bz[0:O_TILES, :], in_=b.rearrange("(t p) -> t p", p=P))
+        nc.scalar.dma_start(out=bb16[0:O_TILES, :], in_=b.rearrange("(t p) -> t p", p=P))
 
         own = N_CHUNKS - 2 - (ON_VECTOR - 1)
 
@@ -182,7 +190,7 @@ def tile_optimalnet_pb_t_kernel(tc, vi, W, b, out_0, out_1):
         mx_in = {}
 
         def prepare(c):
-            due = EARLY_SUMS + 3 * (c - 1) // 2 - taken[0] if c > 1 else 0
+            due = EARLY_SUMS + 12 * (c - 1) // 7 - taken[0] if c > 1 else 0
             banks = transposes(x_tiles[c])
             grouped = in_slot(grouped_slot(c), BF16, "gr%d" % c)
             codes = cp.tile([P, PASSES * CHUNK], U32, name="codes", tag="codes", align_bytes=64)
@@ -255,20 +263,20 @@ def tile_optimalnet_pb_t_kernel(tc, vi, W, b, out_0, out_1):
                         scale=1.0,
                         accum_out=acc[:, ot * N_CHUNKS + c : ot * N_CHUNKS + c + 1],
                     )
-                if c == N_CHUNKS - 2:
-                    nc.vector.tensor_scalar(
-                        out=junk_m[:, 0 : N_CHUNKS - 1],
-                        in0=acc[:, ot * N_CHUNKS : (ot + 1) * N_CHUNKS - 1],
-                        scalar1=1.0,
-                        scalar2=None,
-                        op0=ALU.mult,
-                        op1=ALU.add,
-                        accum_out=part[:, ot : ot + 1],
-                    )
+            if c == N_CHUNKS - 2:
+                nc.vector.tensor_reduce(
+                    out=part[:],
+                    in_=acc[:].rearrange("p (o c) -> p o c", c=N_CHUNKS)[:, :, 0 : N_CHUNKS - 1],
+                    axis=mybir.AxisListType.X,
+                    op=ALU.add,
+                )
 
+        warm_bank = ps.tile([P, OUTS], F32, name="warm", tag="T")
+        for i in range(WARM_UP):
+            keep_clock(warm_bank)
         w_transposes(0, "s")
         w_quantise(0)
-        nc.vector.tensor_copy(out=bzf[:], in_=bz[:])
+        nc.vector.tensor_copy(out=bzf[:], in_=bb16[:])
         prepare(0)
         for ot in range(1, O_TILES):
             w_transposes(ot, "s")
@@ -285,8 +293,9 @@ def tile_optimalnet_pb_t_kernel(tc, vi, W, b, out_0, out_1):
         for i in range(1, N_CHUNKS):
             if i + 1 < N_CHUNKS:
                 prepare(i + 1)
-            if i == N_CHUNKS - 1:
+            if i == N_CHUNKS - 2:
                 row_sums(len(items))
+            if i == N_CHUNKS - 1:
                 nc.vector.tensor_scalar(
                     out=rsc_v[:, 0 : SUB * ON_VECTOR],
                     in0=rs_v[:, 0 : SUB * ON_VECTOR],
@@ -298,6 +307,8 @@ def tile_optimalnet_pb_t_kernel(tc, vi, W, b, out_0, out_1):
 
         def back(c, t, tag):
             bank = ps.tile([P, OUTS], F32, name="bk", tag=tag)
+            if t % 2 == 0:
+                keep_clock(bank)
             for ot in range(O_TILES):
                 block = vj_tiles[c][:, ot * CHUNK + t * P : ot * CHUNK + (t + 1) * P]
                 nc.tensor.transpose(bank[:, ot * P : (ot + 1) * P], block, ident[:])

@@ -53,13 +53,12 @@ def tile_optimalnet_pb_t_kernel(tc, vi, W, b, out_0, out_1):
         acc = const.tile([P, O_TILES * N_CHUNKS], F32, name="acc")
         idle = const.tile([P, OUTS], BF16, name="idle")
         part = const.tile([P, O_TILES], F32, name="part")
-        ident_mean = const.tile([P, P], F32, name="ident_mean")
         mb = const.tile([P, OUTS], F32, name="mb")
         rs_v = const.tile([P, N_CHUNKS * SUB], F32, name="rs_v")
         rsc_v = const.tile([P, N_CHUNKS * SUB], F32, name="rsc_v")
         rsc_s = const.tile([P, N_CHUNKS * SUB], F32, name="rsc_s")
-        w_codes = const.tile([P, PASSES * OUTS], U32, name="w_codes", align_bytes=64)
-        w_planes = const.tile([P, PASSES * OUTS], U8, name="w_planes", align_bytes=64)
+        w_codes = const.tile([P, PASSES * OUTS], U32, name="w_codes", align_bytes=256)
+        w_planes = const.tile([P, PASSES * OUTS], U8, name="w_planes", align_bytes=256)
 
         make_identity(nc, ident[:])
         nc.gpsimd.memset(mb[:], 0.0)
@@ -70,9 +69,6 @@ def tile_optimalnet_pb_t_kernel(tc, vi, W, b, out_0, out_1):
         def keep_clock(bank):
             nc.tensor.matmul(out=bank[:], lhsT=bz[:], rhs=idle[:], start=True, stop=True)
 
-        nc.vector.tensor_scalar(
-            out=ident_mean[:], in0=ident[:], scalar1=1.0 / ROWS, scalar2=None, op0=ALU.mult
-        )
         nc.scalar.dma_start(out=bb16[0:O_TILES, :], in_=b.rearrange("(t p) -> t p", p=P))
 
         own = N_CHUNKS - 2 - (ON_VECTOR - 1)
@@ -193,8 +189,8 @@ def tile_optimalnet_pb_t_kernel(tc, vi, W, b, out_0, out_1):
             due = EARLY_SUMS + 12 * (c - 1) // 7 - taken[0] if c > 1 else 0
             banks = transposes(x_tiles[c])
             grouped = in_slot(grouped_slot(c), BF16, "gr%d" % c)
-            codes = cp.tile([P, PASSES * CHUNK], U32, name="codes", tag="codes", align_bytes=64)
-            planes = cp.tile([P, PASSES * CHUNK], U8, name="planes", tag="planes", align_bytes=64)
+            codes = cp.tile([P, PASSES * CHUNK], U32, name="codes", tag="codes", align_bytes=256)
+            planes = cp.tile([P, PASSES * CHUNK], U8, name="planes", tag="planes", align_bytes=256)
             copy_out("v", grouped, banks, 0)
             copy_out("s", grouped, banks, 2)
             copy_out("v", grouped, banks, 1)
@@ -325,12 +321,15 @@ def tile_optimalnet_pb_t_kernel(tc, vi, W, b, out_0, out_1):
                 nc.tensor.matmul(
                     out=(m_bank_last if ot == last else m_bank)[:, ot * P : (ot + 1) * P],
                     lhsT=sums[h].to_broadcast([P, P]),
-                    rhs=ident_mean[:],
+                    rhs=ident[:],
+                    is_transpose=True,
                     start=(h == 0),
                     stop=(h == 1),
                 )
-        nc.vector.tensor_copy(out=mb[:, 0 : last * P], in_=m_bank[:, 0 : last * P])
-        nc.vector.tensor_copy(out=mb[:, last * P : OUTS], in_=m_bank_last[:, last * P : OUTS])
+        for bank, cols in ((m_bank, slice(0, last * P)), (m_bank_last, slice(last * P, OUTS))):
+            nc.vector.tensor_scalar(
+                out=mb[:, cols], in0=bank[:, cols], scalar1=1.0 / ROWS, scalar2=None, op0=ALU.mult
+            )
         for t in range(1, SUB):
             first.append(back(0, t, "T"))
 
@@ -338,7 +337,7 @@ def tile_optimalnet_pb_t_kernel(tc, vi, W, b, out_0, out_1):
             for t in range(SUB):
                 x_row = x_tiles[c][:, t * K_IN : (t + 1) * K_IN]
                 if t % 2 == 1:
-                    half = cp.tile([P, K_IN // 2], F32, name="half", tag="codes", align_bytes=64)
+                    half = cp.tile([P, K_IN // 2], F32, name="half", tag="codes", align_bytes=256)
                     nc.gpsimd.tensor_tensor(
                         out=half[:], in0=x_row[:, 0 : K_IN // 2], in1=x_row[:, K_IN // 2 : K_IN], op=ALU.add
                     )

@@ -25,7 +25,8 @@ FLOPS = 2 * ROWS * K_IN * OUTS
 
 WARM_UP = 4
 EARLY_SUMS = 2
-DEFERRED = 9
+DEFERRED = 8
+HALVED = 2
 ON_VECTOR = N_CHUNKS - DEFERRED
 SLOT_BYTES = 8192
 
@@ -57,8 +58,8 @@ def tile_optimalnet_pb_t_kernel(tc, vi, W, b, out_0, out_1):
         rs_v = const.tile([P, N_CHUNKS * SUB], F32, name="rs_v")
         rsc_v = const.tile([P, N_CHUNKS * SUB], F32, name="rsc_v")
         rsc_s = const.tile([P, N_CHUNKS * SUB], F32, name="rsc_s")
-        w_codes = const.tile([P, PASSES * OUTS], U32, name="w_codes", align_bytes=256)
-        w_planes = const.tile([P, PASSES * OUTS], U8, name="w_planes", align_bytes=256)
+        w_codes = const.tile([P, PASSES * OUTS], U32, name="w_codes", align_bytes=64)
+        w_planes = const.tile([P, PASSES * OUTS], U8, name="w_planes", align_bytes=64)
 
         make_identity(nc, ident[:])
         nc.gpsimd.memset(mb[:], 0.0)
@@ -186,11 +187,11 @@ def tile_optimalnet_pb_t_kernel(tc, vi, W, b, out_0, out_1):
         mx_in = {}
 
         def prepare(c):
-            due = EARLY_SUMS + 12 * (c - 1) // 7 - taken[0] if c > 1 else 0
+            due = EARLY_SUMS + 27 * (c - 1) // 14 - taken[0] if c > 1 else 0
             banks = transposes(x_tiles[c])
             grouped = in_slot(grouped_slot(c), BF16, "gr%d" % c)
-            codes = cp.tile([P, PASSES * CHUNK], U32, name="codes", tag="codes", align_bytes=256)
-            planes = cp.tile([P, PASSES * CHUNK], U8, name="planes", tag="planes", align_bytes=256)
+            codes = cp.tile([P, PASSES * CHUNK], U32, name="codes", tag="codes", align_bytes=64)
+            planes = cp.tile([P, PASSES * CHUNK], U8, name="planes", tag="planes", align_bytes=64)
             copy_out("v", grouped, banks, 0)
             copy_out("s", grouped, banks, 2)
             copy_out("v", grouped, banks, 1)
@@ -240,7 +241,7 @@ def tile_optimalnet_pb_t_kernel(tc, vi, W, b, out_0, out_1):
                 else:
                     for g in range(PASSES):
                         mx_pass(ot, g)
-                if c == N_CHUNKS - 1 and ot % 2 == 1:
+                if c == N_CHUNKS - 1 and ot == O_TILES - 1:
                     nc.vector.scalar_tensor_tensor(
                         out=vj[:, ot * CHUNK : (ot + 1) * CHUNK],
                         in0=z_banks[ot][:],
@@ -336,8 +337,8 @@ def tile_optimalnet_pb_t_kernel(tc, vi, W, b, out_0, out_1):
         for c in range(ON_VECTOR, N_CHUNKS):
             for t in range(SUB):
                 x_row = x_tiles[c][:, t * K_IN : (t + 1) * K_IN]
-                if t % 2 == 1:
-                    half = cp.tile([P, K_IN // 2], F32, name="half", tag="codes", align_bytes=256)
+                if t % 2 == 1 and c < ON_VECTOR + HALVED:
+                    half = cp.tile([P, K_IN // 2], F32, name="half", tag="codes", align_bytes=64)
                     nc.gpsimd.tensor_tensor(
                         out=half[:], in0=x_row[:, 0 : K_IN // 2], in1=x_row[:, K_IN // 2 : K_IN], op=ALU.add
                     )

from contextlib import ExitStack

import concourse.mybir as mybir
from concourse.masks import make_identity

F32 = mybir.dt.float32
BF16 = mybir.dt.bfloat16
U32 = mybir.dt.uint32
U8 = mybir.dt.uint8
FP8X4 = mybir.dt.float8_e4m3fn_x4
ALU = mybir.AluOpType
ACT = mybir.ActivationFunctionType

P = 128
ROWS = 8192
K_IN = 1024
OUTS = 512
CHUNK = 512
N_CHUNKS = ROWS // CHUNK
SUB = CHUNK // P
O_TILES = OUTS // P
PASSES = K_IN // 512
C_HEBB = 0.01 * 0.001 / 1
FLOPS = 2 * ROWS * K_IN * OUTS

WARM_UP = 4
EARLY_SUMS = 2
DEFERRED = 8
HALVED = 2
ON_VECTOR = N_CHUNKS - DEFERRED
SLOT_BYTES = 8192


def tile_optimalnet_pb_t_kernel(tc, vi, W, b, out_0, out_1):
    nc = tc.nc
    vi_c = vi.rearrange("(c p t) k -> c p (t k)", p=P, t=SUB)
    vi_ct = vi.rearrange("(c p t) k -> c t p k", p=P, t=SUB)
    w_t = W.rearrange("(t p) k -> t p k", p=P)
    out_c = out_0.rearrange("(c p t) o -> c p (t o)", p=P, t=SUB)
    out_ct = out_0.rearrange("(c p t) o -> c t p o", p=P, t=SUB)

    with ExitStack() as ctx:
        const = ctx.enter_context(tc.tile_pool(name="const", bufs=1))
        slots = ctx.enter_context(tc.tile_pool(name="slots", bufs=1))
        cp = ctx.enter_context(tc.tile_pool(name="cp", bufs=2))
        ps = ctx.enter_context(tc.psum_pool(name="ps", bufs=4))
        ctx.enter_context(tc.manual_schedule())

        ident = const.tile([P, P], F32, name="ident")
        bz = const.tile([P, P], BF16, name="bz")
        bb16 = const.tile([P, P], BF16, name="bb16")
        bzf = const.tile([P, P], F32, name="bzf")
        bias = const.tile([P, O_TILES], F32, name="bias")
        acc = const.tile([P, O_TILES * N_CHUNKS], F32, name="acc")
        idle = const.tile([P, OUTS], BF16, name="idle")
        part = const.tile([P, O_TILES], F32, name="part")
        mb = const.tile([P, OUTS], F32, name="mb")
        rs_v = const.tile([P, N_CHUNKS * SUB], F32, name="rs_v")
        rsc_v = const.tile([P, N_CHUNKS * SUB], F32, name="rsc_v")
        rsc_s = const.tile([P, N_CHUNKS * SUB], F32, name="rsc_s")
        w_codes = const.tile([P, PASSES * OUTS], U32, name="w_codes", align_bytes=64)
        w_planes = const.tile([P, PASSES * OUTS], U8, name="w_planes", align_bytes=64)

        make_identity(nc, ident[:])
        nc.gpsimd.memset(mb[:], 0.0)
        nc.vector.memset(bb16[:], 0.0)
        nc.vector.memset(bz[:], 0.0)
        nc.vector.memset(idle[:], 0.0)

        def keep_clock(bank):
            nc.tensor.matmul(out=bank[:], lhsT=bz[:], rhs=idle[:], start=True, stop=True)

        nc.scalar.dma_start(out=bb16[0:O_TILES, :], in_=b.rearrange("(t p) -> t p", p=P))

        own = N_CHUNKS - 2 - (ON_VECTOR - 1)

        def x_slot(c):
            return c - ON_VECTOR if c >= ON_VECTOR else DEFERRED + 1 + c

        def grouped_slot(c):
            return N_CHUNKS + 1 + c % 2

        def vj_slot(c):
            if c >= N_CHUNKS - 2:
                return grouped_slot(c)
            return N_CHUNKS + 3 + c if c < own else DEFERRED + c - own

        def out_slot(c):
            return x_slot(ON_VECTOR - 2 + c) if c < 2 else vj_slot(c - 2)

        def in_slot(slot, dtype, name):
            width = SLOT_BYTES // (2 if dtype == BF16 else 4)
            return slots.tile([P, width], dtype, name=name, tag="slot%d" % slot, align_bytes=64)

        x_tiles = {}

        def load(c):
            x = in_slot(x_slot(c), BF16, "x%d" % c)
            x_tiles[c] = x
            if c == 0:
                for t in range(SUB):
                    nc.sync.dma_start(out=x[:, t * K_IN : (t + 1) * K_IN], in_=vi_ct[c, t])
            else:
                nc.sync.dma_start(out=x[:], in_=vi_c[c])

        def transposes(x):
            x32 = x[:].bitcast(F32)
            banks = {}
            for tp in range(2):
                for g in range(PASSES):
                    bank = ps.tile([P, 512], F32, name="tb", tag="T")
                    for tt in range(2):
                        t = 2 * tp + tt
                        for u in range(2):
                            col = 512 * t + 128 * (2 * g + u)
                            nc.tensor.transpose(
                                bank[:, 256 * u + 128 * tt : 256 * u + 128 * tt + 128],
                                x32[:, col : col + 128],
                                ident[:],
                            )
                    banks[2 * g + tp] = bank
            return banks

        def copy(engine, dst, src):
            if engine == "v":
                nc.vector.tensor_copy(out=dst, in_=src)
            else:
                nc.scalar.copy(out=dst, in_=src)

        def copy_out(engine, grouped, banks, j):
            g32 = grouped[:].bitcast(F32)
            dst = g32[:, 512 * j : 512 * j + 512].rearrange("p (c u) -> p c u", u=2)
            src = banks[j][:].rearrange("p (u c) -> p c u", u=2)
            copy(engine, dst, src)

        items = [(c, t) for c in range(ON_VECTOR) for t in range(SUB)]
        taken = [0]

        def row_sums(n):
            for q in range(n):
                if taken[0] < len(items):
                    c, t = items[taken[0]]
                    taken[0] = taken[0] + 1
                    nc.vector.tensor_scalar(
                        out=x_tiles[c][:, t * K_IN : (t + 1) * K_IN],
                        in0=x_tiles[c][:, t * K_IN : (t + 1) * K_IN],
                        scalar1=1.0,
                        scalar2=None,
                        op0=ALU.mult,
                        op1=ALU.add,
                        accum_out=rs_v[:, SUB * c + t : SUB * c + t + 1],
                    )

        wx = in_slot(DEFERRED, BF16, "wx")
        nc.sync.dma_start(out=wx[:, 0:K_IN], in_=w_t[0])
        load(0)
        for t in range(1, O_TILES):
            nc.sync.dma_start(out=wx[:, t * K_IN : (t + 1) * K_IN], in_=w_t[t])
        for c in range(1, N_CHUNKS):
            load(c)

        w_grouped = in_slot(grouped_slot(1), BF16, "wg")
        wx32 = wx[:].bitcast(F32)
        wg32 = w_grouped[:].bitcast(F32)

        def w_transposes(ot, engine):
            bank = ps.tile([P, 512], F32, name="wb", tag="Z")
            for q in range(4):
                nc.tensor.transpose(
                    bank[:, 128 * q : 128 * q + 128],
                    wx32[:, 512 * ot + 128 * q : 512 * ot + 128 * q + 128],
                    ident[:],
                )
            copy(
                engine,
                wg32[:, 512 * ot : 512 * ot + 512].rearrange("p (g c u) -> p g c u", g=2, u=2),
                bank[:].rearrange("p (g u c) -> p g c u", g=2, u=2),
            )

        def w_quantise(ot):
            nc.vector.quantize_mx(
                out=w_codes[:, 256 * ot : 256 * ot + 256].bitcast(FP8X4),
                scales=w_planes[:, 256 * ot : 256 * ot + 256],
                in_=w_grouped[:, 1024 * ot : 1024 * ot + 1024],
            )

        mx_in = {}

        def prepare(c):
            due = EARLY_SUMS + 27 * (c - 1) // 14 - taken[0] if c > 1 else 0
            banks = transposes(x_tiles[c])
            grouped = in_slot(grouped_slot(c), BF16, "gr%d" % c)
            codes = cp.tile([P, PASSES * CHUNK], U32, name="codes", tag="codes", align_bytes=64)
            planes = cp.tile([P, PASSES * CHUNK], U8, name="planes", tag="planes", align_bytes=64)
            copy_out("v", grouped, banks, 0)
            copy_out("s", grouped, banks, 2)
            copy_out("v", grouped, banks, 1)
            copy_out("s", grouped, banks, 3)
            row_sums(due // 2)
            if c < 2:
                for g in range(PASSES):
                    cols = slice(g * CHUNK, (g + 1) * CHUNK)
                    nc.vector.quantize_mx(
                        out=codes[:, cols].bitcast(FP8X4),
                        scales=planes[:, cols],
                        in_=grouped[:, 4 * g * CHUNK : 4 * (g + 1) * CHUNK],
                    )
            else:
                nc.vector.quantize_mx(out=codes[:].bitcast(FP8X4), scales=planes[:], in_=grouped[:])
            row_sums(due - due // 2)
            mx_in[c] = (codes, planes)

        vj_tiles = {}

        def multiply(c):
            codes, planes = mx_in[c]
            vj = in_slot(vj_slot(c), F32, "vj%d" % c)
            vj_tiles[c] = vj
            z_banks = {}

            def mx_pass(ot, g):
                if g == 0:
                    z_banks[ot] = ps.tile([P, CHUNK], F32, name="z", tag="Z")
                w0 = 256 * ot + 128 * g
                nc.tensor.matmul_mx(
                    out=z_banks[ot][:],
                    lhsT=w_codes[:, w0 : w0 + P].bitcast(FP8X4),
                    lhsT_scale=w_planes[:, w0 : w0 + P],
                    rhs=codes[:, g * CHUNK : (g + 1) * CHUNK].bitcast(FP8X4),
                    rhs_scale=planes[:, g * CHUNK : (g + 1) * CHUNK],
                    start=(g == 0),
                    stop=(g == PASSES - 1),
                )

            for ot in range(O_TILES):
                if c == 1 and ot < 2:
                    if ot == 0:
                        mx_pass(0, 0)
                        mx_pass(1, 0)
                    mx_pass(ot, 1)
                else:
                    for g in range(PASSES):
                        mx_pass(ot, g)
                if c == N_CHUNKS - 1 and ot == O_TILES - 1:
                    nc.vector.scalar_tensor_tensor(
                        out=vj[:, ot * CHUNK : (ot + 1) * CHUNK],
                        in0=z_banks[ot][:],
                        scalar=bias[:, ot : ot + 1],
                        in1=mb[:],
                        op0=ALU.add,
                        op1=ALU.max,
                        accum_out=acc[:, ot * N_CHUNKS + c : ot * N_CHUNKS + c + 1],
                    )
                else:
                    nc.scalar.activation(
                        out=vj[:, ot * CHUNK : (ot + 1) * CHUNK],
                        in_=z_banks[ot][:],
                        func=ACT.Relu,
                        bias=bias[:, ot : ot + 1],
                        scale=1.0,
                        accum_out=acc[:, ot * N_CHUNKS + c : ot * N_CHUNKS + c + 1],
                    )
            if c == N_CHUNKS - 2:
                nc.vector.tensor_reduce(
                    out=part[:],
                    in_=acc[:].rearrange("p (o c) -> p o c", c=N_CHUNKS)[:, :, 0 : N_CHUNKS - 1],
                    axis=mybir.AxisListType.X,
                    op=ALU.add,
                )

        warm_bank = ps.tile([P, OUTS], F32, name="warm", tag="T")
        for i in range(WARM_UP):
            keep_clock(warm_bank)
        w_transposes(0, "s")
        w_quantise(0)
        nc.vector.tensor_copy(out=bzf[:], in_=bb16[:])
        prepare(0)
        for ot in range(1, O_TILES):
            w_transposes(ot, "s")
        b_bank = ps.tile([P, 512], F32, name="bb", tag="T")
        nc.tensor.transpose(b_bank[:, 0:P], bzf[:], ident[:])
        w_quantise(1)
        nc.vector.tensor_copy(out=bias[:], in_=b_bank[:, 0:O_TILES])
        w_quantise(2)
        w_quantise(3)
        row_sums(EARLY_SUMS)

        multiply(0)
        prepare(1)
        for i in range(1, N_CHUNKS):
            if i + 1 < N_CHUNKS:
                prepare(i + 1)
            if i == N_CHUNKS - 2:
                row_sums(len(items))
            if i == N_CHUNKS - 1:
                nc.vector.tensor_scalar(
                    out=rsc_v[:, 0 : SUB * ON_VECTOR],
                    in0=rs_v[:, 0 : SUB * ON_VECTOR],
                    scalar1=C_HEBB,
                    scalar2=None,
                    op0=ALU.mult,
                )
            multiply(i)

        def back(c, t, tag):
            bank = ps.tile([P, OUTS], F32, name="bk", tag=tag)
            if t % 2 == 0:
                keep_clock(bank)
            for ot in range(O_TILES):
                block = vj_tiles[c][:, ot * CHUNK + t * P : ot * CHUNK + (t + 1) * P]
                nc.tensor.transpose(bank[:, ot * P : (ot + 1) * P], block, ident[:])
            return bank

        first = [back(0, 0, "T")]

        m_bank = ps.tile([P, OUTS], F32, name="mbk", tag="Z")
        m_bank_last = ps.tile([P, OUTS], F32, name="mbl", tag="Z")
        last = O_TILES - 1
        for ot in range(O_TILES):
            sums = [part[:, ot : ot + 1], acc[:, (ot + 1) * N_CHUNKS - 1 : (ot + 1) * N_CHUNKS]]
            for h in range(2):
                nc.tensor.matmul(
                    out=(m_bank_last if ot == last else m_bank)[:, ot * P : (ot + 1) * P],
                    lhsT=sums[h].to_broadcast([P, P]),
                    rhs=ident[:],
                    is_transpose=True,
                    start=(h == 0),
                    stop=(h == 1),
                )
        for bank, cols in ((m_bank, slice(0, last * P)), (m_bank_last, slice(last * P, OUTS))):
            nc.vector.tensor_scalar(
                out=mb[:, cols], in0=bank[:, cols], scalar1=1.0 / ROWS, scalar2=None, op0=ALU.mult
            )
        for t in range(1, SUB):
            first.append(back(0, t, "T"))

        for c in range(ON_VECTOR, N_CHUNKS):
            for t in range(SUB):
                x_row = x_tiles[c][:, t * K_IN : (t + 1) * K_IN]
                if t % 2 == 1 and c < ON_VECTOR + HALVED:
                    half = cp.tile([P, K_IN // 2], F32, name="half", tag="codes", align_bytes=64)
                    nc.gpsimd.tensor_tensor(
                        out=half[:], in0=x_row[:, 0 : K_IN // 2], in1=x_row[:, K_IN // 2 : K_IN], op=ALU.add
                    )
                    x_row = half[:]
                nc.scalar.activation(
                    out=x_row,
                    in_=x_row,
                    func=ACT.Copy,
                    scale=C_HEBB,
                    accum_out=rsc_s[:, SUB * c + t : SUB * c + t + 1],
                )
        nc.gpsimd.dma_start(out=out_1.rearrange("(a o) -> a o", a=1), in_=mb[0:1, :])

        for c in range(N_CHUNKS):
            stage = in_slot(out_slot(c), F32, "st%d" % c)
            rsc = rsc_v if c < ON_VECTOR else rsc_s
            for t in range(SUB):
                bank = first[t] if c == 0 else back(c, t, "T" if c % 2 == 0 else "Z")
                nc.vector.scalar_tensor_tensor(
                    out=stage[:, t * OUTS : (t + 1) * OUTS],
                    in0=mb[:],
                    scalar=rsc[:, SUB * c + t : SUB * c + t + 1],
                    in1=bank[:],
                    op0=ALU.mult,
                    op1=ALU.add,
                )
                if c == 0 or c == N_CHUNKS - 1:
                    nc.sync.dma_start(out=out_ct[c, t], in_=stage[:, t * OUTS : (t + 1) * OUTS])
                elif t % 2 == 1:
                    nc.sync.dma_start(
                        out=out_c[c][:, (t - 1) * OUTS : (t + 1) * OUTS],
                        in_=stage[:, (t - 1) * OUTS : (t + 1) * OUTS],
                    )
